import numpy as np
import ml_dtypes


def mxq(x, axis, fmt="e4m3"):
    dtype, down = {"e4m3": (ml_dtypes.float8_e4m3fn, 7), "e5m2": (ml_dtypes.float8_e5m2, 14)}[fmt]
    v = np.moveaxis(np.asarray(x, np.float32).astype(ml_dtypes.bfloat16).astype(np.float64), axis, -1)
    blocks = v.reshape(v.shape[:-1] + (-1, 32))
    amax = np.abs(blocks).max(-1, keepdims=True)
    byte = np.maximum(np.where(amax > 0, np.frexp(amax)[1] - 1 + 127, 0) - down, 1)
    scale = np.exp2(byte - 127.0)
    codes = (blocks / scale).astype(np.float32).astype(dtype).astype(np.float64)
    return np.moveaxis((codes * scale).reshape(v.shape), -1, axis)


WIDE = False


def mx_kscale(k):
    if not WIDE:
        return np.ones(k)
    levels = np.array([30, -30])
    if k % 512:
        return np.exp2(np.random.permutation(np.resize(levels, k // 32))).repeat(32)
    a = np.empty((k // 512, 16))
    for p in range(k // 512):
        a[p, :8] = np.random.permutation(np.resize(levels, 8))
        for g in range(8):
            far = levels[np.abs(levels - a[p, g]) >= 10]
            a[p, g + 8] = far[np.random.randint(len(far))]
    return np.exp2(a.ravel()).repeat(32)


BF16 = ml_dtypes.bfloat16


def bf(x):
    return np.asarray(x, np.float32).astype(BF16)


def f64(x):
    return np.asarray(x).astype(np.float64)


B, S, D, NH, NKV, HD, W, QB = 1, 1024, 1024, 8, 4, 128, 256, 512
THETA = 10000.0


def rope(u, c, s):
    ur, ui = u[..., ::2], u[..., 1::2]
    return np.stack([ur * c - ui * s, ur * s + ui * c], axis=-1).reshape(u.shape)


def setup_inputs():
    s = mx_kscale(D)
    fr = np.outer(np.arange(S), 1.0 / THETA ** (np.arange(0, HD, 2) / HD))
    return {"x": bf(np.random.standard_normal((B, S, D)) * s),
            "freqs_cos": bf(np.cos(fr)),
            "freqs_sin": bf(np.sin(fr)),
            "wq": bf(np.random.standard_normal((D, NH * HD)) * 1.4 / np.sqrt(D) / s[:, None]),
            "wk": bf(np.random.standard_normal((D, NKV * HD)) * 1.4 / np.sqrt(D) / s[:, None]),
            "wv": bf(np.random.standard_normal((D, NKV * HD)) / np.sqrt(D) / s[:, None])}


def reference(x, freqs_cos, freqs_sin, wq, wk, wv):
    xm = mxq(f64(x), 2, "e5m2")
    xq = (xm @ mxq(f64(wq), 0, "e5m2")).reshape(B, S, NH, HD)
    xk = (xm @ mxq(f64(wk), 0, "e5m2")).reshape(B, S, NKV, HD)
    xv = (xm @ mxq(f64(wv), 0, "e5m2")).reshape(B, S, NKV, HD)
    fc, fs = f64(freqs_cos), f64(freqs_sin)
    cos = fc[:S][None, :, None, :]
    sin = fs[:S][None, :, None, :]
    q1 = rope(xq, cos, sin)
    k1 = rope(xk, cos, sin)
    q2 = rope(xq, fc[W][None, None, None, :], fs[W][None, None, None, :])
    return q1, q2, k1, xk, xv

@@ -1,0 +1,332 @@
+from contextlib import ExitStack
+
+import concourse.mybir as mybir
+from concourse.masks import make_identity
+
+S, D, NH, NKV, HD, W = 1024, 1024, 8, 4, 128, 256
+FLOPS = 2 * S * D * (NH + 2 * NKV) * HD
+
+F32 = mybir.dt.float32
+BF16 = mybir.dt.bfloat16
+U32 = mybir.dt.uint32
+U8 = mybir.dt.uint8
+E5M2X4 = mybir.dt.float8_e5m2_x4
+MULT = mybir.AluOpType.mult
+ADD = mybir.AluOpType.add
+
+P = 128
+PACK = 4
+K_PASS = P * PACK
+PASSES = D // K_PASS
+TILES = S // P
+PAIRS = TILES // 2
+BANK = 512
+HEADS_PER_BANK = BANK // HD
+HALF = HD // 2
+
+PE_HEADS = 6
+VCOLS = [512, 512, 0, 0, 512, 256, 0, 0]
+SPLIT = 1
+DIGIT = {"0": 0, "1": 1, "2": 2, "3": 3}
+VADD = [(1, 3, 1)]
+WADD = [3]
+LOADS = "x0 a0 x1 a1 t w2 x2 x3 w1 w3"
+PIECE = 128
+VB = 4
+SB = 4
+ORDER = "X0 G00 w00 X1 x0 G01 S0 w01 x1 g213 C00 G20 G21 w20 g212 W0 w21 C01 T00 X2 g100 g101 T20 x2 l0 h00 R00 g102 X3 g103 r00 i00 k0 g110 T01 C02 x3 g111 T21 l1 h01 g112 R01 g113 r01 i01 k1 T02 y1 C03 g300 T22 l2 h02 g301 R02 g302 r02 i02 k2 g303 T03 C10 g310 w30 T23 l3 h03 g311 g312 R03 g313 C11 r03 i03 k3 w31 T10 R10 C12 V0 v0 h10 i10 T11 R11 C13 V1 v1 h11 T12 V2 v2 i11 R12 T13 V3 v3 h12 i12 R13 h13 i13"
+
+
+def tile_attention_pa_kernel(tc, x, freqs_cos, freqs_sin, wq, wk, wv, out_0, out_1, out_2, out_3, out_4):
+    nc = tc.nc
+    x_v = x.rearrange("b (p t) d -> p (b t) d", t=TILES)
+    q1_v, q2_v, k1_v, k2_v, v_v = [
+        o.rearrange("b (p t) h d -> p (b t) (h d)", t=TILES) for o in (out_0, out_1, out_2, out_3, out_4)
+    ]
+    w_cols = [wq[:, 0:BANK], wq[:, BANK : 2 * BANK], wk, wv]
+
+    with ExitStack() as ctx:
+        keep = ctx.enter_context(tc.tile_pool(name="keep", bufs=1))
+        work = ctx.enter_context(tc.tile_pool(name="work", bufs=3))
+        psum = ctx.enter_context(tc.psum_pool(name="psum", bufs=1))
+        ctx.enter_context(tc.manual_schedule())
+
+        ident = keep.tile([P, P], F32, name="ident")
+        pick = keep.tile([P, P], BF16, name="pick")
+        cos_sb = keep.tile([P, TILES, HALF], BF16, name="cos_sb")
+        sin_sb = keep.tile([P, 2, TILES, HALF], BF16, name="sin_sb")
+        sin2 = keep.tile([P, TILES, HALF, 2], BF16, name="sin2")
+        cos_w = keep.tile([P, HALF], F32, name="cos_w")
+        sin2_w = keep.tile([P, HALF, 2], F32, name="sin2_w")
+        rot_a = keep.tile([P, HD], F32, name="rot_a")
+        rot_b = keep.tile([P, HD], F32, name="rot_b")
+        rot_w = keep.tile([P, HD], F32, name="rot_w")
+        x_raw = [keep.tile([P, 2, D], BF16, name="x_raw%d" % i) for i in range(PAIRS)]
+        w_raw = [[keep.tile([P, PACK, BANK], BF16, name="w_raw%d_%d" % (b, g)) for g in range(PASSES)] for b in range(4)]
+        x_codes = [keep.tile([P, PASSES, 2, P], U32, name="x_codes%d" % i, align_bytes=64) for i in range(PAIRS)]
+        x_scales = [keep.tile([P, PASSES, 2, P], U8, name="x_scales%d" % i, align_bytes=64) for i in range(PAIRS)]
+        w_codes = [keep.tile([P, PASSES, BANK], U32, name="w_codes%d" % b, align_bytes=64) for b in range(4)]
+        w_scales = [keep.tile([P, PASSES, BANK], U8, name="w_scales%d" % b, align_bytes=64) for b in range(4)]
+        staged = {}
+        grouped = {}
+        turned = {}
+        held = {}
+
+        def load_x(tp):
+            nc.sync.dma_start(out=x_raw[tp][:], in_=x_v[:, 2 * tp : 2 * tp + 2, :])
+
+        def load_w(b, passes):
+            for g in passes:
+                rows = w_cols[b][g * K_PASS : (g + 1) * K_PASS, :]
+                nc.sync.dma_start(out=w_raw[b][g][:], in_=rows.rearrange("(p j) n -> p j n", j=PACK))
+
+        def turn_x(tp):
+            xg = work.tile([P, PASSES, 2, P, PACK], BF16, name="x_grouped", bufs=2, align_bytes=64)
+            grouped["x", tp] = xg
+            for i in range(2):
+                words = x_raw[tp][:, i, :].bitcast(F32)
+                xt = psum.tile([P, PASSES, 2, P], F32, name="s_bank", bufs=SB)
+                for g in range(PASSES):
+                    for u in range(2):
+                        nc.tensor.transpose(xt[:, g, u, :], words[:, 256 * g + u : 256 * (g + 1) : 2], ident[:])
+                nc.scalar.copy(out=xg[:, :, i, :, :].bitcast(F32), in_=xt[:].rearrange("p g u r -> p g r u"))
+
+        def quantize_x(tp):
+            nc.vector.quantize_mx(
+                out=x_codes[tp][:].rearrange("p g i r -> p (g i r)").bitcast(E5M2X4),
+                scales=x_scales[tp][:].rearrange("p g i r -> p (g i r)"),
+                in_=grouped["x", tp][:].rearrange("p g i r j -> p (g i r j)"),
+            )
+
+        def group_cols(b, g, c0, c1, copy):
+            if b not in grouped:
+                grouped[b] = work.tile([P, PASSES, BANK, PACK], BF16, name="w_grouped", bufs=2, align_bytes=64)
+            src = w_raw[b][g][:].rearrange("p j (c i) -> p c j i", i=4)
+            dst = grouped[b][:, g].rearrange("p (c i) j -> p c j i", i=4)
+            copy(out=dst[:, c0 // 4 : c1 // 4], in_=src[:, c0 // 4 : c1 // 4])
+
+        def group_w(b, g):
+            group_cols(b, g, 0, VCOLS[PASSES * b + g], nc.vector.tensor_copy)
+
+        def group_piece(b, g, q):
+            group_cols(b, g, q * PIECE, (q + 1) * PIECE, nc.scalar.copy)
+
+        def quantize_w(b, g0, g1):
+            nc.vector.quantize_mx(
+                out=w_codes[b][:, g0:g1].rearrange("p g n -> p (g n)").bitcast(E5M2X4),
+                scales=w_scales[b][:, g0:g1].rearrange("p g n -> p (g n)"),
+                in_=grouped[b][:, g0:g1].rearrange("p g n j -> p (g n j)"),
+            )
+
+        def project(b, tp, i, acc, c1):
+            for g in range(PASSES):
+                nc.tensor.matmul_mx(
+                    out=acc[:, c1:BANK],
+                    lhsT=x_codes[tp][:, g, i, :].bitcast(E5M2X4),
+                    lhsT_scale=x_scales[tp][:, g, i, :],
+                    rhs=w_codes[b][:, g, c1:BANK].bitcast(E5M2X4),
+                    rhs_scale=w_scales[b][:, g, c1:BANK],
+                    start=(g == 0),
+                    stop=(g == PASSES - 1),
+                )
+
+        def project_turned(b, tp, h, acc):
+            cols = slice(h * HD, (h + 1) * HD)
+            for g in range(PASSES):
+                nc.tensor.matmul_mx(
+                    out=acc,
+                    lhsT=w_codes[b][:, g, cols].bitcast(E5M2X4),
+                    lhsT_scale=w_scales[b][:, g, cols],
+                    rhs=x_codes[tp][:, g, :, :].rearrange("p i r -> p (i r)").bitcast(E5M2X4),
+                    rhs_scale=x_scales[tp][:, g, :, :].rearrange("p i r -> p (i r)"),
+                    start=(g == 0),
+                    stop=(g == PASSES - 1),
+                )
+
+        def products(u, cos, sin_pairs, first, second):
+            heads = u.shape[1] // HD
+            shape = [P, heads, HALF, 2]
+            pairs = u.rearrange("p (h m two) -> p h m two", m=HALF, two=2)
+            nc.vector.tensor_tensor(
+                out=first.rearrange("p (h m two) -> p h m two", m=HALF, two=2),
+                in0=pairs,
+                in1=cos.unsqueeze(1).unsqueeze(3).to_broadcast(shape),
+                op=MULT,
+            )
+            nc.vector.tensor_tensor(
+                out=second.rearrange("p (h m two) -> p h m two", m=HALF, two=2),
+                in0=pairs[:, :, :, ::-1],
+                in1=sin_pairs.unsqueeze(1).to_broadcast(shape),
+                op=MULT,
+            )
+
+        def stage(kind, tp, width, bufs):
+            if (kind, tp) not in staged:
+                staged[kind, tp] = work.tile([P, 2, width], F32, name=kind, bufs=bufs)
+            return staged[kind, tp]
+
+        def heads_on_pe(b):
+            return min(HEADS_PER_BANK, PE_HEADS - b * HEADS_PER_BANK)
+
+        def by_token(b, tp):
+            c0 = 0
+            first = stage("k1", tp, BANK, 4) if b == 2 else stage("q1", (b, tp), BANK, 4)
+            second = work.tile([P, 2, BANK], F32, name="second", bufs=3)
+            on_pe = 0 if b == 2 else heads_on_pe(b)
+            c1 = on_pe * HD
+            window = b < 2 and c1 < BANK
+            if window:
+                q2 = stage("q2", (b, tp), BANK, 4)
+                second_w = work.tile([P, 2, BANK - c1], F32, name="second_w", bufs=2)
+            accs = []
+            for i in range(2):
+                acc = psum.tile([P, BANK], F32, name="v_bank", bufs=VB)
+                accs.append(acc)
+                if c1 < BANK:
+                    project(b, tp, i, acc, c1)
+            held[b, tp] = accs
+            if b == 2:
+                keys_plain(tp)
+            for i in range(2):
+                acc = accs[i]
+                for h in range(on_pe):
+                    nc.tensor.transpose(acc[:, h * HD : (h + 1) * HD], turned[b, tp, h // 2][:, h % 2, i * P : (i + 1) * P], ident[:])
+            for i in range(2):
+                acc = accs[i]
+                t = 2 * tp + i
+                products(acc[:], cos_sb[:, t, :], sin2[:, t, :, :], first[:, i, c0 : c0 + BANK], second[:, i, :])
+                if SPLIT:
+                    (nc.vector if (b, tp, i) in VADD else nc.gpsimd).tensor_tensor(out=first[:, i, c0 : c0 + BANK], in0=first[:, i, c0 : c0 + BANK], in1=second[:, i, :], op=ADD)
+                if window:
+                    products(acc[:, c1:BANK], cos_w[:], sin2_w[:], q2[:, i, c0 + c1 : c0 + BANK], second_w[:, i, :])
+            if not SPLIT:
+                dst = first[:, :, c0 : c0 + BANK]
+                nc.gpsimd.tensor_tensor(out=dst, in0=dst, in1=second[:], op=ADD)
+            if window:
+                dst = q2[:, :, c0 + c1 : c0 + BANK]
+                (nc.vector if tp in WADD else nc.gpsimd).tensor_tensor(out=dst, in0=dst, in1=second_w[:], op=ADD)
+
+        def keys_plain(tp):
+            k2 = stage("k2", tp, BANK, 4)
+            for i in range(2):
+                nc.scalar.copy(out=k2[:, i, :], in_=held[2, tp][i][:])
+
+        def by_channel(b, tp):
+            on_pe = heads_on_pe(b)
+            for h0 in range(0, on_pe, 2):
+                nh = min(2, on_pe - h0)
+                acc = psum.tile([P, 2, 2 * P], F32, name="s_bank", bufs=SB)
+                for h in range(nh):
+                    project_turned(b, tp, h0 + h, acc[:, h, :])
+                ut = work.tile([P, 2, 2 * P], F32, name="turned", bufs=6)
+                nc.scalar.copy(out=ut[:, 0:nh, :], in_=acc[:, 0:nh, :])
+                turned[b, tp, h0 // 2] = ut
+
+        def window_rotate(b, tp, parts):
+            q2 = stage("q2", (b, tp), BANK, 4)
+            c0 = 0
+            on_pe = heads_on_pe(b)
+            per_bank = 2 if on_pe <= 2 else 1
+            for i0 in parts:
+                acc = psum.tile([P, per_bank, on_pe * HD], F32, name="s_bank", bufs=SB)
+                for i in range(per_bank):
+                    for h in range(on_pe):
+                        nc.tensor.matmul(
+                            out=acc[:, i, h * HD : (h + 1) * HD],
+                            lhsT=turned[b, tp, h // 2][:, h % 2, (i0 + i) * P : (i0 + i + 1) * P],
+                            rhs=rot_w[:],
+                            start=True,
+                            stop=True,
+                        )
+                nc.scalar.copy(out=q2[:, i0 : i0 + per_bank, c0 : c0 + on_pe * HD], in_=acc[:])
+
+        def values(tp):
+            v = stage("v", tp, BANK, 4)
+            for i in range(2):
+                acc = psum.tile([P, BANK], F32, name="s_bank", bufs=SB)
+                project(3, tp, i, acc, 0)
+                nc.scalar.copy(out=v[:, i, :], in_=acc[:])
+
+        def store(kind, tp, c0, c1, key):
+            dst = {"q1": q1_v, "q2": q2_v, "k1": k1_v, "k2": k2_v, "v": v_v}[kind]
+            nc.sync.dma_start(out=dst[:, 2 * tp : 2 * tp + 2, c0:c1], in_=staged[kind, key][:])
+
+        def sine_pairs():
+            nc.vector.tensor_scalar_mul(out=sin_sb[:, 0], in0=sin_sb[:, 1], scalar1=-1.0)
+            nc.scalar.copy(out=sin2[:], in_=sin_sb[:].rearrange("p two t m -> p t m two"))
+
+        def window_rotation():
+            acc = psum.tile([P, HALF + HD], F32, name="v_bank", bufs=VB)
+            t = W % TILES
+            nc.tensor.matmul(out=acc[:, 0:HALF], lhsT=pick[:], rhs=cos_sb[:, t, :], start=True, stop=True)
+            nc.tensor.matmul(
+                out=acc[:, HALF : HALF + HD],
+                lhsT=pick[:],
+                rhs=sin2[:, t, :, :].rearrange("p m two -> p (m two)"),
+                start=True,
+                stop=True,
+            )
+            sin_pairs = acc[:, HALF : HALF + HD].rearrange("p (m two) -> p m two", two=2)
+            nc.scalar.copy(out=cos_w[:], in_=acc[:, 0:HALF])
+            nc.scalar.copy(out=sin2_w[:], in_=sin_pairs)
+            products(ident[:], acc[:, 0:HALF], sin_pairs, rot_a[:], rot_b[:])
+            nc.gpsimd.tensor_tensor(out=rot_w[:], in0=rot_a[:], in1=rot_b[:], op=ADD)
+
+        for word in LOADS.split():
+            if word == "t":
+                nc.sync.dma_start(out=sin_sb[:, 1], in_=freqs_sin.rearrange("(p t) m -> p t m", t=TILES))
+                nc.sync.dma_start(out=cos_sb[:], in_=freqs_cos.rearrange("(p t) m -> p t m", t=TILES))
+            elif word[0] == "x":
+                load_x(DIGIT[word[1]])
+            elif word[0] == "a":
+                load_w(0, [DIGIT[word[1]]])
+            else:
+                load_w(DIGIT[word[1]], range(PASSES))
+
+        nc.gpsimd.memset(pick[:], 0.0)
+        row = W // TILES
+        nc.gpsimd.memset(pick[row : row + 1, :], 1.0)
+        make_identity(nc, ident[:])
+
+        for word in ORDER.split():
+            op = word[0]
+            a = DIGIT[word[1]]
+            b = DIGIT[word[2:3] or "0"]
+            if op == "S":
+                sine_pairs()
+            elif op == "W":
+                window_rotation()
+            elif op == "X":
+                turn_x(a)
+            elif op == "x":
+                quantize_x(a)
+            elif op == "G":
+                group_w(a, b)
+            elif op == "w":
+                quantize_w(a, b, b + 1)
+            elif op == "y":
+                quantize_w(a, 0, PASSES)
+            elif op == "T":
+                by_token(a, b)
+            elif op == "C":
+                by_channel(a, b)
+            elif op == "R":
+                window_rotate(a, b, [0])
+            elif op == "u":
+                keys_plain(a)
+            elif op == "r":
+                window_rotate(a, b, [1])
+            elif op == "g":
+                group_piece(a, b, DIGIT[word[3]])
+            elif op == "V":
+                values(a)
+            elif op == "h":
+                store("q1", b, a * BANK, (a + 1) * BANK, (a, b))
+            elif op == "i":
+                store("q2", b, a * BANK, (a + 1) * BANK, (a, b))
+            elif op == "k":
+                store("k1", a, 0, BANK, a)
+            elif op == "l":
+                store("k2", a, 0, BANK, a)
+            else:
+                store("v", a, 0, BANK, a)

@@ -25,16 +25,17 @@ HEADS_PER_BANK = BANK // HD
 HALF = HD // 2
 
 PE_HEADS = 6
-VCOLS = [512, 512, 0, 0, 512, 256, 0, 0]
-SPLIT = 1
+VCOLS = [512, 512, 0, 0, 512, 512, 0, 0]
+SPLIT = 0
+VUNIT = []
 DIGIT = {"0": 0, "1": 1, "2": 2, "3": 3}
 VADD = [(1, 3, 1)]
 WADD = [3]
-LOADS = "x0 a0 x1 a1 t w2 x2 x3 w1 w3"
+LOADS = "a0 x0 a1 x1 t w2 x2 x3 w1 w3"
 PIECE = 128
 VB = 4
 SB = 4
-ORDER = "X0 G00 w00 X1 x0 G01 S0 w01 x1 g213 C00 G20 G21 w20 g212 W0 w21 C01 T00 X2 g100 g101 T20 x2 l0 h00 R00 g102 X3 g103 r00 i00 k0 g110 T01 C02 x3 g111 T21 l1 h01 g112 R01 g113 r01 i01 k1 T02 y1 C03 g300 T22 l2 h02 g301 R02 g302 r02 i02 k2 g303 T03 C10 g310 w30 T23 l3 h03 g311 g312 R03 g313 C11 r03 i03 k3 w31 T10 R10 C12 V0 v0 h10 i10 T11 R11 C13 V1 v1 h11 T12 V2 v2 i11 R12 T13 V3 v3 h12 i12 R13 h13 i13"
+ORDER = "G00 w00 X0 G01 w01 x0 X1 S0 G20 x1 C00 G21 w20 w21 W0 C01 g100 T00 T20 X2 x2 h00 g101 R00 g102 X3 u0 l0 g103 r00 k0 i00 g110 T01 C02 x3 g111 T21 h01 g112 R01 g113 u1 l1 r01 k1 i01 T02 y1 C03 g300 T22 h02 g301 R02 g302 u2 l2 r02 i02 k2 g303 T03 C10 g310 T23 h03 g311 C11 g312 T10 g313 u3 l3 R03 r03 k3 i03 y3 R10 C12 T11 h10 i10 R11 C13 T12 V0 v0 V1 v1 h11 i11 R12 T13 V2 v2 h12 i12 R13 V3 v3 h13 i13"
 
 
 def tile_attention_pa_kernel(tc, x, freqs_cos, freqs_sin, wq, wk, wv, out_0, out_1, out_2, out_3, out_4):
@@ -185,8 +186,6 @@ def tile_attention_pa_kernel(tc, x, freqs_cos, freqs_sin, wq, wk, wv, out_0, out
                 if c1 < BANK:
                     project(b, tp, i, acc, c1)
             held[b, tp] = accs
-            if b == 2:
-                keys_plain(tp)
             for i in range(2):
                 acc = accs[i]
                 for h in range(on_pe):
@@ -201,7 +200,7 @@ def tile_attention_pa_kernel(tc, x, freqs_cos, freqs_sin, wq, wk, wv, out_0, out
                     products(acc[:, c1:BANK], cos_w[:], sin2_w[:], q2[:, i, c0 + c1 : c0 + BANK], second_w[:, i, :])
             if not SPLIT:
                 dst = first[:, :, c0 : c0 + BANK]
-                nc.gpsimd.tensor_tensor(out=dst, in0=dst, in1=second[:], op=ADD)
+                (nc.vector if (b, tp) in VUNIT else nc.gpsimd).tensor_tensor(out=dst, in0=dst, in1=second[:], op=ADD)
             if window:
                 dst = q2[:, :, c0 + c1 : c0 + BANK]
                 (nc.vector if tp in WADD else nc.gpsimd).tensor_tensor(out=dst, in0=dst, in1=second_w[:], op=ADD)
@@ -267,8 +266,8 @@ def tile_attention_pa_kernel(tc, x, freqs_cos, freqs_sin, wq, wk, wv, out_0, out
                 stop=True,
             )
             sin_pairs = acc[:, HALF : HALF + HD].rearrange("p (m two) -> p m two", two=2)
-            nc.scalar.copy(out=cos_w[:], in_=acc[:, 0:HALF])
-            nc.scalar.copy(out=sin2_w[:], in_=sin_pairs)
+            nc.vector.tensor_copy(out=cos_w[:], in_=acc[:, 0:HALF])
+            nc.vector.tensor_copy(out=sin2_w[:], in_=sin_pairs)
             products(ident[:], acc[:, 0:HALF], sin_pairs, rot_a[:], rot_b[:])
             nc.gpsimd.tensor_tensor(out=rot_w[:], in0=rot_a[:], in1=rot_b[:], op=ADD)
 

from contextlib import ExitStack

import concourse.mybir as mybir
from concourse.masks import make_identity

S, D, NH, NKV, HD, W = 1024, 1024, 8, 4, 128, 256
FLOPS = 2 * S * D * (NH + 2 * NKV) * HD

F32 = mybir.dt.float32
BF16 = mybir.dt.bfloat16
U32 = mybir.dt.uint32
U8 = mybir.dt.uint8
E5M2X4 = mybir.dt.float8_e5m2_x4
MULT = mybir.AluOpType.mult
ADD = mybir.AluOpType.add

P = 128
PACK = 4
K_PASS = P * PACK
PASSES = D // K_PASS
TILES = S // P
PAIRS = TILES // 2
BANK = 512
HEADS_PER_BANK = BANK // HD
HALF = HD // 2

PE_HEADS = 6
VCOLS = [512, 512, 0, 0, 512, 512, 0, 0]
SPLIT = 0
VUNIT = []
DIGIT = {"0": 0, "1": 1, "2": 2, "3": 3}
VADD = [(1, 3, 1)]
WADD = [3]
LOADS = "a0 x0 a1 x1 t w2 x2 x3 w1 w3"
PIECE = 128
VB = 4
SB = 4
ORDER = "G00 w00 X0 G01 w01 x0 X1 S0 G20 x1 C00 G21 w20 w21 W0 C01 g100 T00 T20 X2 x2 h00 g101 R00 g102 X3 u0 l0 g103 r00 k0 i00 g110 T01 C02 x3 g111 T21 h01 g112 R01 g113 u1 l1 r01 k1 i01 T02 y1 C03 g300 T22 h02 g301 R02 g302 u2 l2 r02 i02 k2 g303 T03 C10 g310 T23 h03 g311 C11 g312 T10 g313 u3 l3 R03 r03 k3 i03 y3 R10 C12 T11 h10 i10 R11 C13 T12 V0 v0 V1 v1 h11 i11 R12 T13 V2 v2 h12 i12 R13 V3 v3 h13 i13"


def tile_attention_pa_kernel(tc, x, freqs_cos, freqs_sin, wq, wk, wv, out_0, out_1, out_2, out_3, out_4):
    nc = tc.nc
    x_v = x.rearrange("b (p t) d -> p (b t) d", t=TILES)
    q1_v, q2_v, k1_v, k2_v, v_v = [
        o.rearrange("b (p t) h d -> p (b t) (h d)", t=TILES) for o in (out_0, out_1, out_2, out_3, out_4)
    ]
    w_cols = [wq[:, 0:BANK], wq[:, BANK : 2 * BANK], wk, wv]

    with ExitStack() as ctx:
        keep = ctx.enter_context(tc.tile_pool(name="keep", bufs=1))
        work = ctx.enter_context(tc.tile_pool(name="work", bufs=3))
        psum = ctx.enter_context(tc.psum_pool(name="psum", bufs=1))
        ctx.enter_context(tc.manual_schedule())

        ident = keep.tile([P, P], F32, name="ident")
        pick = keep.tile([P, P], BF16, name="pick")
        cos_sb = keep.tile([P, TILES, HALF], BF16, name="cos_sb")
        sin_sb = keep.tile([P, 2, TILES, HALF], BF16, name="sin_sb")
        sin2 = keep.tile([P, TILES, HALF, 2], BF16, name="sin2")
        cos_w = keep.tile([P, HALF], F32, name="cos_w")
        sin2_w = keep.tile([P, HALF, 2], F32, name="sin2_w")
        rot_a = keep.tile([P, HD], F32, name="rot_a")
        rot_b = keep.tile([P, HD], F32, name="rot_b")
        rot_w = keep.tile([P, HD], F32, name="rot_w")
        x_raw = [keep.tile([P, 2, D], BF16, name="x_raw%d" % i) for i in range(PAIRS)]
        w_raw = [[keep.tile([P, PACK, BANK], BF16, name="w_raw%d_%d" % (b, g)) for g in range(PASSES)] for b in range(4)]
        x_codes = [keep.tile([P, PASSES, 2, P], U32, name="x_codes%d" % i, align_bytes=64) for i in range(PAIRS)]
        x_scales = [keep.tile([P, PASSES, 2, P], U8, name="x_scales%d" % i, align_bytes=64) for i in range(PAIRS)]
        w_codes = [keep.tile([P, PASSES, BANK], U32, name="w_codes%d" % b, align_bytes=64) for b in range(4)]
        w_scales = [keep.tile([P, PASSES, BANK], U8, name="w_scales%d" % b, align_bytes=64) for b in range(4)]
        staged = {}
        grouped = {}
        turned = {}
        held = {}

        def load_x(tp):
            nc.sync.dma_start(out=x_raw[tp][:], in_=x_v[:, 2 * tp : 2 * tp + 2, :])

        def load_w(b, passes):
            for g in passes:
                rows = w_cols[b][g * K_PASS : (g + 1) * K_PASS, :]
                nc.sync.dma_start(out=w_raw[b][g][:], in_=rows.rearrange("(p j) n -> p j n", j=PACK))

        def turn_x(tp):
            xg = work.tile([P, PASSES, 2, P, PACK], BF16, name="x_grouped", bufs=2, align_bytes=64)
            grouped["x", tp] = xg
            for i in range(2):
                words = x_raw[tp][:, i, :].bitcast(F32)
                xt = psum.tile([P, PASSES, 2, P], F32, name="s_bank", bufs=SB)
                for g in range(PASSES):
                    for u in range(2):
                        nc.tensor.transpose(xt[:, g, u, :], words[:, 256 * g + u : 256 * (g + 1) : 2], ident[:])
                nc.scalar.copy(out=xg[:, :, i, :, :].bitcast(F32), in_=xt[:].rearrange("p g u r -> p g r u"))

        def quantize_x(tp):
            nc.vector.quantize_mx(
                out=x_codes[tp][:].rearrange("p g i r -> p (g i r)").bitcast(E5M2X4),
                scales=x_scales[tp][:].rearrange("p g i r -> p (g i r)"),
                in_=grouped["x", tp][:].rearrange("p g i r j -> p (g i r j)"),
            )

        def group_cols(b, g, c0, c1, copy):
            if b not in grouped:
                grouped[b] = work.tile([P, PASSES, BANK, PACK], BF16, name="w_grouped", bufs=2, align_bytes=64)
            src = w_raw[b][g][:].rearrange("p j (c i) -> p c j i", i=4)
            dst = grouped[b][:, g].rearrange("p (c i) j -> p c j i", i=4)
            copy(out=dst[:, c0 // 4 : c1 // 4], in_=src[:, c0 // 4 : c1 // 4])

        def group_w(b, g):
            group_cols(b, g, 0, VCOLS[PASSES * b + g], nc.vector.tensor_copy)

        def group_piece(b, g, q):
            group_cols(b, g, q * PIECE, (q + 1) * PIECE, nc.scalar.copy)

        def quantize_w(b, g0, g1):
            nc.vector.quantize_mx(
                out=w_codes[b][:, g0:g1].rearrange("p g n -> p (g n)").bitcast(E5M2X4),
                scales=w_scales[b][:, g0:g1].rearrange("p g n -> p (g n)"),
                in_=grouped[b][:, g0:g1].rearrange("p g n j -> p (g n j)"),
            )

        def project(b, tp, i, acc, c1):
            for g in range(PASSES):
                nc.tensor.matmul_mx(
                    out=acc[:, c1:BANK],
                    lhsT=x_codes[tp][:, g, i, :].bitcast(E5M2X4),
                    lhsT_scale=x_scales[tp][:, g, i, :],
                    rhs=w_codes[b][:, g, c1:BANK].bitcast(E5M2X4),
                    rhs_scale=w_scales[b][:, g, c1:BANK],
                    start=(g == 0),
                    stop=(g == PASSES - 1),
                )

        def project_turned(b, tp, h, acc):
            cols = slice(h * HD, (h + 1) * HD)
            for g in range(PASSES):
                nc.tensor.matmul_mx(
                    out=acc,
                    lhsT=w_codes[b][:, g, cols].bitcast(E5M2X4),
                    lhsT_scale=w_scales[b][:, g, cols],
                    rhs=x_codes[tp][:, g, :, :].rearrange("p i r -> p (i r)").bitcast(E5M2X4),
                    rhs_scale=x_scales[tp][:, g, :, :].rearrange("p i r -> p (i r)"),
                    start=(g == 0),
                    stop=(g == PASSES - 1),
                )

        def products(u, cos, sin_pairs, first, second):
            heads = u.shape[1] // HD
            shape = [P, heads, HALF, 2]
            pairs = u.rearrange("p (h m two) -> p h m two", m=HALF, two=2)
            nc.vector.tensor_tensor(
                out=first.rearrange("p (h m two) -> p h m two", m=HALF, two=2),
                in0=pairs,
                in1=cos.unsqueeze(1).unsqueeze(3).to_broadcast(shape),
                op=MULT,
            )
            nc.vector.tensor_tensor(
                out=second.rearrange("p (h m two) -> p h m two", m=HALF, two=2),
                in0=pairs[:, :, :, ::-1],
                in1=sin_pairs.unsqueeze(1).to_broadcast(shape),
                op=MULT,
            )

        def stage(kind, tp, width, bufs):
            if (kind, tp) not in staged:
                staged[kind, tp] = work.tile([P, 2, width], F32, name=kind, bufs=bufs)
            return staged[kind, tp]

        def heads_on_pe(b):
            return min(HEADS_PER_BANK, PE_HEADS - b * HEADS_PER_BANK)

        def by_token(b, tp):
            c0 = 0
            first = stage("k1", tp, BANK, 4) if b == 2 else stage("q1", (b, tp), BANK, 4)
            second = work.tile([P, 2, BANK], F32, name="second", bufs=3)
            on_pe = 0 if b == 2 else heads_on_pe(b)
            c1 = on_pe * HD
            window = b < 2 and c1 < BANK
            if window:
                q2 = stage("q2", (b, tp), BANK, 4)
                second_w = work.tile([P, 2, BANK - c1], F32, name="second_w", bufs=2)
            accs = []
            for i in range(2):
                acc = psum.tile([P, BANK], F32, name="v_bank", bufs=VB)
                accs.append(acc)
                if c1 < BANK:
                    project(b, tp, i, acc, c1)
            held[b, tp] = accs
            for i in range(2):
                acc = accs[i]
                for h in range(on_pe):
                    nc.tensor.transpose(acc[:, h * HD : (h + 1) * HD], turned[b, tp, h // 2][:, h % 2, i * P : (i + 1) * P], ident[:])
            for i in range(2):
                acc = accs[i]
                t = 2 * tp + i
                products(acc[:], cos_sb[:, t, :], sin2[:, t, :, :], first[:, i, c0 : c0 + BANK], second[:, i, :])
                if SPLIT:
                    (nc.vector if (b, tp, i) in VADD else nc.gpsimd).tensor_tensor(out=first[:, i, c0 : c0 + BANK], in0=first[:, i, c0 : c0 + BANK], in1=second[:, i, :], op=ADD)
                if window:
                    products(acc[:, c1:BANK], cos_w[:], sin2_w[:], q2[:, i, c0 + c1 : c0 + BANK], second_w[:, i, :])
            if not SPLIT:
                dst = first[:, :, c0 : c0 + BANK]
                (nc.vector if (b, tp) in VUNIT else nc.gpsimd).tensor_tensor(out=dst, in0=dst, in1=second[:], op=ADD)
            if window:
                dst = q2[:, :, c0 + c1 : c0 + BANK]
                (nc.vector if tp in WADD else nc.gpsimd).tensor_tensor(out=dst, in0=dst, in1=second_w[:], op=ADD)

        def keys_plain(tp):
            k2 = stage("k2", tp, BANK, 4)
            for i in range(2):
                nc.scalar.copy(out=k2[:, i, :], in_=held[2, tp][i][:])

        def by_channel(b, tp):
            on_pe = heads_on_pe(b)
            for h0 in range(0, on_pe, 2):
                nh = min(2, on_pe - h0)
                acc = psum.tile([P, 2, 2 * P], F32, name="s_bank", bufs=SB)
                for h in range(nh):
                    project_turned(b, tp, h0 + h, acc[:, h, :])
                ut = work.tile([P, 2, 2 * P], F32, name="turned", bufs=6)
                nc.scalar.copy(out=ut[:, 0:nh, :], in_=acc[:, 0:nh, :])
                turned[b, tp, h0 // 2] = ut

        def window_rotate(b, tp, parts):
            q2 = stage("q2", (b, tp), BANK, 4)
            c0 = 0
            on_pe = heads_on_pe(b)
            per_bank = 2 if on_pe <= 2 else 1
            for i0 in parts:
                acc = psum.tile([P, per_bank, on_pe * HD], F32, name="s_bank", bufs=SB)
                for i in range(per_bank):
                    for h in range(on_pe):
                        nc.tensor.matmul(
                            out=acc[:, i, h * HD : (h + 1) * HD],
                            lhsT=turned[b, tp, h // 2][:, h % 2, (i0 + i) * P : (i0 + i + 1) * P],
                            rhs=rot_w[:],
                            start=True,
                            stop=True,
                        )
                nc.scalar.copy(out=q2[:, i0 : i0 + per_bank, c0 : c0 + on_pe * HD], in_=acc[:])

        def values(tp):
            v = stage("v", tp, BANK, 4)
            for i in range(2):
                acc = psum.tile([P, BANK], F32, name="s_bank", bufs=SB)
                project(3, tp, i, acc, 0)
                nc.scalar.copy(out=v[:, i, :], in_=acc[:])

        def store(kind, tp, c0, c1, key):
            dst = {"q1": q1_v, "q2": q2_v, "k1": k1_v, "k2": k2_v, "v": v_v}[kind]
            nc.sync.dma_start(out=dst[:, 2 * tp : 2 * tp + 2, c0:c1], in_=staged[kind, key][:])

        def sine_pairs():
            nc.vector.tensor_scalar_mul(out=sin_sb[:, 0], in0=sin_sb[:, 1], scalar1=-1.0)
            nc.scalar.copy(out=sin2[:], in_=sin_sb[:].rearrange("p two t m -> p t m two"))

        def window_rotation():
            acc = psum.tile([P, HALF + HD], F32, name="v_bank", bufs=VB)
            t = W % TILES
            nc.tensor.matmul(out=acc[:, 0:HALF], lhsT=pick[:], rhs=cos_sb[:, t, :], start=True, stop=True)
            nc.tensor.matmul(
                out=acc[:, HALF : HALF + HD],
                lhsT=pick[:],
                rhs=sin2[:, t, :, :].rearrange("p m two -> p (m two)"),
                start=True,
                stop=True,
            )
            sin_pairs = acc[:, HALF : HALF + HD].rearrange("p (m two) -> p m two", two=2)
            nc.vector.tensor_copy(out=cos_w[:], in_=acc[:, 0:HALF])
            nc.vector.tensor_copy(out=sin2_w[:], in_=sin_pairs)
            products(ident[:], acc[:, 0:HALF], sin_pairs, rot_a[:], rot_b[:])
            nc.gpsimd.tensor_tensor(out=rot_w[:], in0=rot_a[:], in1=rot_b[:], op=ADD)

        for word in LOADS.split():
            if word == "t":
                nc.sync.dma_start(out=sin_sb[:, 1], in_=freqs_sin.rearrange("(p t) m -> p t m", t=TILES))
                nc.sync.dma_start(out=cos_sb[:], in_=freqs_cos.rearrange("(p t) m -> p t m", t=TILES))
            elif word[0] == "x":
                load_x(DIGIT[word[1]])
            elif word[0] == "a":
                load_w(0, [DIGIT[word[1]]])
            else:
                load_w(DIGIT[word[1]], range(PASSES))

        nc.gpsimd.memset(pick[:], 0.0)
        row = W // TILES
        nc.gpsimd.memset(pick[row : row + 1, :], 1.0)
        make_identity(nc, ident[:])

        for word in ORDER.split():
            op = word[0]
            a = DIGIT[word[1]]
            b = DIGIT[word[2:3] or "0"]
            if op == "S":
                sine_pairs()
            elif op == "W":
                window_rotation()
            elif op == "X":
                turn_x(a)
            elif op == "x":
                quantize_x(a)
            elif op == "G":
                group_w(a, b)
            elif op == "w":
                quantize_w(a, b, b + 1)
            elif op == "y":
                quantize_w(a, 0, PASSES)
            elif op == "T":
                by_token(a, b)
            elif op == "C":
                by_channel(a, b)
            elif op == "R":
                window_rotate(a, b, [0])
            elif op == "u":
                keys_plain(a)
            elif op == "r":
                window_rotate(a, b, [1])
            elif op == "g":
                group_piece(a, b, DIGIT[word[3]])
            elif op == "V":
                values(a)
            elif op == "h":
                store("q1", b, a * BANK, (a + 1) * BANK, (a, b))
            elif op == "i":
                store("q2", b, a * BANK, (a + 1) * BANK, (a, b))
            elif op == "k":
                store("k1", a, 0, BANK, a)
            elif op == "l":
                store("k2", a, 0, BANK, a)
            else:
                store("v", a, 0, BANK, a)
